import numpy as np
import ml_dtypes


def mxq(x, axis, fmt="e4m3"):
    dtype, down = {"e4m3": (ml_dtypes.float8_e4m3fn, 7), "e5m2": (ml_dtypes.float8_e5m2, 14)}[fmt]
    v = np.moveaxis(np.asarray(x, np.float32).astype(ml_dtypes.bfloat16).astype(np.float64), axis, -1)
    blocks = v.reshape(v.shape[:-1] + (-1, 32))
    amax = np.abs(blocks).max(-1, keepdims=True)
    byte = np.maximum(np.where(amax > 0, np.frexp(amax)[1] - 1 + 127, 0) - down, 1)
    scale = np.exp2(byte - 127.0)
    codes = (blocks / scale).astype(np.float32).astype(dtype).astype(np.float64)
    return np.moveaxis((codes * scale).reshape(v.shape), -1, axis)


WIDE = False


def mx_kscale(k):
    if not WIDE:
        return np.ones(k)
    levels = np.array([30, -30])
    if k % 512:
        return np.exp2(np.random.permutation(np.resize(levels, k // 32))).repeat(32)
    a = np.empty((k // 512, 16))
    for p in range(k // 512):
        a[p, :8] = np.random.permutation(np.resize(levels, 8))
        for g in range(8):
            far = levels[np.abs(levels - a[p, g]) >= 10]
            a[p, g + 8] = far[np.random.randint(len(far))]
    return np.exp2(a.ravel()).repeat(32)


BF16 = ml_dtypes.bfloat16


def bf(x):
    return np.asarray(x, np.float32).astype(BF16)


def f64(x):
    return np.asarray(x).astype(np.float64)


N, I0, O0, I1, O1, I2, O2, D0, D1, D2 = 1024, 512, 512, 256, 256, 128, 128, 1, 3, 5


def irrep_linear(x, w):
    return (x.transpose(2, 0, 1) @ w.transpose(2, 1, 0)).transpose(1, 2, 0)


def setup_inputs():
    s = mx_kscale(I0)
    return {"x0e": bf(np.random.standard_normal((N, I0, D0)) * s[None, :, None]),
            "x1o": bf(np.random.standard_normal((N, I1, D1))),
            "x2e": bf(np.random.standard_normal((N, I2, D2))),
            "w0e": bf(np.random.standard_normal((O0, I0, D0)) / np.sqrt(I0) / s[None, :, None]),
            "w1o": bf(np.random.standard_normal((O1, I1, D1)) / np.sqrt(I1)),
            "w2e": bf(np.random.standard_normal((O2, I2, D2)) / np.sqrt(I2)),
            "bias": bf(np.random.standard_normal(O0) * 0.5)}


def reference(x0e, x1o, x2e, w0e, w1o, w2e, bias):
    y0e = irrep_linear(mxq(f64(x0e), 1, "e5m2"), mxq(f64(w0e), 1, "e5m2")) + f64(bias)[None, :, None]
    y1o = irrep_linear(f64(x1o), f64(w1o))
    y2e = irrep_linear(f64(x2e), f64(w2e))
    n = x0e.shape[0]
    return np.concatenate([y0e.reshape(n, -1), y1o.reshape(n, -1), y2e.reshape(n, -1)], axis=-1)

@@ -1,0 +1,292 @@
+from contextlib import ExitStack
+
+import concourse.mybir as mybir
+from concourse.masks import make_identity
+
+F32 = mybir.dt.float32
+BF16 = mybir.dt.bfloat16
+U32 = mybir.dt.uint32
+U8 = mybir.dt.uint8
+FP8X4 = mybir.dt.float8_e5m2_x4
+ADD = mybir.AluOpType.add
+MULT = mybir.AluOpType.mult
+
+P = 128
+ROWS = 1024
+CHUNKS = 4
+K0 = 512
+O0 = 512
+I1, O1, D1 = 256, 256, 3
+I2, O2, D2 = 128, 128, 5
+W1 = I1 * D1
+W2 = I2 * D2
+NB1 = 6
+NB2 = 5
+Y1 = O0
+Y2 = O0 + O1 * D1
+WIDTH = Y2 + O2 * D2
+
+POOL_CHUNKS = ()
+WARM = 0
+ACT_2E = ((0, 0),)
+DVE_1O = ()
+
+FLOPS = 2 * ROWS * (K0 * O0 + D1 * I1 * O1 + D2 * I2 * O2)
+
+
+def tile_linearlayer_kernel(tc, x0e, x1o, x2e, w0e, w1o, w2e, bias, out):
+    nc = tc.nc
+    with ExitStack() as ctx:
+        keep = ctx.enter_context(tc.tile_pool(name="keep", bufs=1))
+        psum_t = ctx.enter_context(tc.psum_pool(name="psum_t", bufs=3))
+        psum_a = ctx.enter_context(tc.psum_pool(name="psum_a", bufs=5))
+        ctx.enter_context(tc.manual_schedule())
+
+        ident_f = keep.tile([P, P], F32, name="ident_f")
+        make_identity(nc, ident_f[:])
+        ones = keep.tile([P, P], BF16, name="ones")
+        nc.gpsimd.memset(ones[:], 1.0)
+        ident_b = keep.tile([P, P], BF16, name="ident_b")
+        make_identity(nc, ident_b[:])
+        bias_row = keep.tile([P, O0], BF16, name="bias_row")
+        nc.vector.memset(bias_row[:], 0.0)
+        warm_in = keep.tile([P, 8], F32, name="warm_in")
+        nc.vector.memset(warm_in[:], 0.0)
+        warm_out = keep.tile([P, 8], F32, name="warm_out")
+        nc.scalar.copy(out=warm_out[:], in_=warm_in[:])
+        if WARM:
+            zeros = keep.tile([P, 512], BF16, name="zeros")
+            nc.vector.memset(zeros[:], 0.0)
+            for i in range(WARM):
+                dummy = psum_a.tile([P, 512], F32, name="acc", tag="acc")
+                nc.tensor.matmul(out=dummy[:], lhsT=ones[:], rhs=zeros[:], start=True, stop=True)
+
+        x0_view = x0e.rearrange("(c t p) k o -> c p t (k o)", c=CHUNKS, t=2, p=P)
+        x1_view = x1o.rearrange("(c p j) i m -> c p (j i m)", c=CHUNKS, p=P, j=2)
+        x2_view = x2e.rearrange("(c p j) i m -> c p (j i m)", c=CHUNKS, p=P, j=2)
+        w0_view = w0e.rearrange("(b t p) k o -> b p t (k o)", b=2, t=2, p=P)
+
+        w0_raw = []
+        for b in range(2):
+            w0_raw.append(keep.tile([P, 2, K0], BF16, name="w0_raw%d" % b))
+        x0_raw, x1_raw, x2_raw = [], [], []
+        x0_grouped, x0_codes, x0_scales, x_pair, x_t, o_tiles = [], [], [], [], [], []
+        for c in range(CHUNKS):
+            x0_raw.append(keep.tile([P, 2, K0], BF16, name="x0_raw%d" % c))
+            x1_raw.append(keep.tile([P, 2 * W1], BF16, name="x1_raw%d" % c))
+            x2_raw.append(keep.tile([P, 2 * W2], BF16, name="x2_raw%d" % c))
+            x0_grouped.append(keep.tile([P, 1024], BF16, name="x0_grouped%d" % c, align_bytes=64))
+            x0_codes.append(keep.tile([P, 256], U32, name="x0_codes%d" % c, align_bytes=64))
+            x0_scales.append(keep.tile([P, 256], U8, name="x0_scales%d" % c, align_bytes=64))
+            x_pair.append(keep.tile([P, 2 * (W1 + W2)], BF16, name="x_pair%d" % c))
+            x_t.append(keep.tile([P, 2 * (W1 + W2)], BF16, name="x_t%d" % c))
+            for h in range(2):
+                o_tiles.append(keep.tile([P, WIDTH], F32, name="o_%d_%d" % (c, h)))
+        w1_raw = keep.tile([P, 2 * W1], BF16, name="w1_raw")
+        w2_raw = keep.tile([P, W2], BF16, name="w2_raw")
+        w1_pair = keep.tile([P, 2 * W1], BF16, name="w1_pair")
+        w0_grouped = keep.tile([P, 4 * O0], BF16, name="w0_grouped", align_bytes=64)
+        w0_codes = keep.tile([P, O0], U32, name="w0_codes", align_bytes=64)
+        w0_scales = keep.tile([P, O0], U8, name="w0_scales", align_bytes=64)
+        w2_t = keep.tile([P, W2], BF16, name="w2_t")
+        w1_t = keep.tile([P, 2 * W1], BF16, name="w1_t")
+        bias_bc = keep.tile([P, O0], F32, name="bias_bc")
+
+        def load_w0(b):
+            nc.sync.dma_start(out=w0_raw[b][:], in_=w0_view[b, :, :, :])
+
+        def load_x0(c):
+            nc.sync.dma_start(out=x0_raw[c][:], in_=x0_view[c, :, :, :])
+
+        def load_x1(c):
+            nc.sync.dma_start(out=x1_raw[c][:], in_=x1_view[c, :, :])
+
+        def load_x2(c):
+            nc.sync.dma_start(out=x2_raw[c][:], in_=x2_view[c, :, :])
+
+        load_w0(0)
+        nc.sync.dma_start(out=w1_raw[:], in_=w1o.rearrange("(p j) i m -> p (j i m)", j=2))
+        load_w0(1)
+        load_x0(0)
+        load_x1(0)
+        nc.sync.dma_start(out=w2_raw[:], in_=w2e.rearrange("o i m -> o (i m)"))
+        load_x2(0)
+        nc.sync.dma_start(out=bias_row[0:1, :], in_=bias.rearrange("(a n) -> a n", a=1))
+        for c in range(1, CHUNKS):
+            load_x1(c)
+            load_x2(c)
+            load_x0(c)
+
+        def pair_rows(eng, dst, src, comps, m0, m1):
+            per = dst.shape[1] // comps
+            o_ap = dst[:, m0 * per : m1 * per].rearrange("p (m i j) -> p m i j", m=m1 - m0, j=2)
+            i_ap = src.rearrange("p (j i m) -> p m i j", j=2, m=comps)[:, m0:m1]
+            if eng == "v":
+                nc.vector.tensor_copy(out=o_ap, in_=i_ap)
+            elif eng == "a":
+                nc.scalar.copy(out=o_ap, in_=i_ap)
+            else:
+                nc.gpsimd.tensor_scalar(out=o_ap, in0=i_ap, scalar1=1.0, scalar2=0.0, op0=MULT, op1=ADD)
+
+        def pair_pieces(c):
+            d1 = x_pair[c][:, 0 : 2 * W1]
+            d2 = x_pair[c][:, 2 * W1 : 2 * (W1 + W2)]
+            s1 = x1_raw[c][:]
+            s2 = x2_raw[c][:]
+            if c in POOL_CHUNKS:
+                return [
+                    lambda: pair_rows("g", d1, s1, D1, 0, D1),
+                    lambda: pair_rows("g", d2, s2, D2, 0, D2),
+                ]
+            return [
+                lambda: pair_rows("v", d1, s1, D1, 0, 2),
+                lambda: pair_rows("v", d1, s1, D1, 2, 3),
+                lambda: pair_rows("v", d2, s2, D2, 0, 4),
+                lambda: pair_rows("v", d2, s2, D2, 4, 5),
+            ]
+
+        def transpose_blocks(src_words, first, count, dst_words):
+            bank = psum_t.tile([P, 512], F32, name="tp", tag="tp")
+            for q in range(count):
+                k = first + q
+                nc.tensor.transpose(bank[:, q * P : (q + 1) * P], src_words[:, k * P : (k + 1) * P], ident_f[:])
+            nc.scalar.copy(out=dst_words[:, first * P : (first + count) * P], in_=bank[:, 0 : count * P])
+
+        def transpose_k(src, grouped):
+            words = src[:].bitcast(F32)
+            bank = psum_t.tile([P, 512], F32, name="tp", tag="tp")
+            for t in range(2):
+                for u in range(2):
+                    q = 2 * t + u
+                    nc.tensor.transpose(bank[:, q * P : (q + 1) * P], words[:, t, u : K0 // 2 : 2], ident_f[:])
+            nc.scalar.copy(
+                out=grouped.bitcast(F32).rearrange("p (t n u) -> p t n u", t=2, u=2),
+                in_=bank[:].rearrange("p (t u n) -> p t n u", t=2, u=2),
+            )
+
+        def quantize(grouped, codes, scales):
+            nc.vector.quantize_mx(out=codes.bitcast(FP8X4), scales=scales, in_=grouped)
+
+        def quantize_w0(b):
+            quantize(
+                w0_grouped[:, b * 1024 : (b + 1) * 1024],
+                w0_codes[:, b * 256 : (b + 1) * 256],
+                w0_scales[:, b * 256 : (b + 1) * 256],
+            )
+
+        def t_bank(c, b):
+            if b == 0:
+                transpose_k(x0_raw[c], x0_grouped[c][:])
+                quantize(x0_grouped[c][:], x0_codes[c][:], x0_scales[c][:])
+            else:
+                first = 4 * (b - 1)
+                count = min(4, NB1 + NB2 - first)
+                transpose_blocks(x_pair[c][:].bitcast(F32), first, count, x_t[c][:].bitcast(F32))
+
+        transpose_k(w0_raw[0], w0_grouped[:, 0:1024])
+        pair_rows("v", w1_pair[:], w1_raw[:], D1, 0, 2)
+        pair_rows("v", w1_pair[:], w1_raw[:], D1, 2, 3)
+        transpose_k(w0_raw[1], w0_grouped[:, 1024:2048])
+        quantize_w0(0)
+        transpose_k(x0_raw[0], x0_grouped[0][:])
+        quantize_w0(1)
+        transpose_blocks(w1_pair[:].bitcast(F32), 0, 4, w1_t[:].bitcast(F32))
+        transpose_blocks(w1_pair[:].bitcast(F32), 4, 2, w1_t[:].bitcast(F32))
+        first_pieces = pair_pieces(0)
+        first_pieces[0]()
+        first_pieces[1]()
+        quantize(x0_grouped[0][:], x0_codes[0][:], x0_scales[0][:])
+
+        bank_b = psum_t.tile([P, W2], BF16, name="tpb", tag="tp")
+        for m in range(D2):
+            nc.tensor.transpose(bank_b[:, m * P : (m + 1) * P], w2_raw[:, m : W2 : D2], ident_b[:])
+        nc.scalar.copy(out=w2_t[:], in_=bank_b[:])
+        for piece in first_pieces[2:]:
+            piece()
+
+        bias_ps = psum_a.tile([P, 512], F32, name="acc", tag="acc")
+        nc.tensor.matmul(out=bias_ps[:], lhsT=ones[:], rhs=bias_row[:], start=True, stop=True)
+        nc.vector.tensor_copy(out=bias_bc[:], in_=bias_ps[:])
+
+        for b in range(1, 4):
+            t_bank(0, b)
+        for piece in pair_pieces(1):
+            piece()
+
+        def mx_group(c, h):
+            acc = psum_a.tile([P, 512], F32, name="acc", tag="acc")
+            cols = slice(h * P, (h + 1) * P)
+            nc.tensor.matmul_mx(
+                out=acc[:],
+                lhsT=x0_codes[c][:, cols].bitcast(FP8X4),
+                lhsT_scale=x0_scales[c][:, cols],
+                rhs=w0_codes[:].bitcast(FP8X4),
+                rhs_scale=w0_scales[:],
+                start=True,
+                stop=True,
+            )
+            nc.vector.tensor_tensor(out=o_tiles[2 * c + h][:, 0:O0], in0=acc[:], in1=bias_bc[:], op=ADD)
+
+        def group_1o(c, h, g):
+            acc = psum_a.tile([P, 512], F32, name="acc", tag="acc")
+            for m in range(D1):
+                for ib in range(2):
+                    k = 2 * m + ib
+                    nc.tensor.matmul(
+                        out=acc[:, m * P : (m + 1) * P],
+                        lhsT=x_t[c][:, k * 256 + h * P : k * 256 + (h + 1) * P],
+                        rhs=w1_t[:, k * 256 + g * P : k * 256 + (g + 1) * P],
+                        start=(ib == 0),
+                        stop=(ib == 1),
+                    )
+            n = D1 * P
+            dst = o_tiles[2 * c + h][:, Y1 + g * n : Y1 + (g + 1) * n]
+            src = acc[:, 0:n].rearrange("p (m o) -> p o m", m=D1)
+            if (h, g) in DVE_1O:
+                nc.vector.tensor_copy(out=dst, in_=src)
+            else:
+                nc.scalar.copy(out=dst, in_=src)
+
+        def group_2e(c, h, g):
+            acc = psum_a.tile([P, 512], F32, name="acc", tag="acc")
+            for m in range(D2):
+                k = NB1 + m
+                nc.tensor.matmul(
+                    out=acc[:, m * 64 : (m + 1) * 64],
+                    lhsT=x_t[c][:, k * 256 + h * P : k * 256 + (h + 1) * P],
+                    rhs=w2_t[:, m * P + g * 64 : m * P + (g + 1) * 64],
+                    start=True,
+                    stop=True,
+                )
+            n = D2 * 64
+            dst = o_tiles[2 * c + h][:, Y2 + g * n : Y2 + (g + 1) * n]
+            src = acc[:, 0:n].rearrange("p (m o) -> p o m", m=D2)
+            if (h, g) in ACT_2E:
+                nc.scalar.copy(out=dst, in_=src)
+            else:
+                nc.vector.tensor_copy(out=dst, in_=src)
+
+        def store(c, h, lo, hi):
+            r0 = (2 * c + h) * P
+            nc.sync.dma_start(out=out[r0 : r0 + P, lo:hi], in_=o_tiles[2 * c + h][:, lo:hi])
+
+        for c in range(CHUNKS):
+            nxt = c + 1 < CHUNKS
+            pieces = pair_pieces(c + 2) if c + 2 < CHUNKS else []
+            per_slot = (len(pieces) + 3) // 4
+            for h in range(2):
+                for piece in pieces[(2 * h) * per_slot : (2 * h + 1) * per_slot]:
+                    piece()
+                if nxt:
+                    t_bank(c + 1, 2 * h)
+                group_1o(c, h, 0)
+                mx_group(c, h)
+                group_1o(c, h, 1)
+                store(c, h, 0, Y2)
+                for piece in pieces[(2 * h + 1) * per_slot : (2 * h + 2) * per_slot]:
+                    piece()
+                if nxt:
+                    t_bank(c + 1, 2 * h + 1)
+                group_2e(c, h, 0)
+                group_2e(c, h, 1)
+                store(c, h, Y2, WIDTH)

@@ -27,7 +27,7 @@ Y2 = O0 + O1 * D1
 WIDTH = Y2 + O2 * D2
 
 POOL_CHUNKS = ()
-WARM = 0
+WARM = 7
 ACT_2E = ((0, 0),)
 DVE_1O = ()
 
@@ -42,6 +42,8 @@ def tile_linearlayer_kernel(tc, x0e, x1o, x2e, w0e, w1o, w2e, bias, out):
         psum_a = ctx.enter_context(tc.psum_pool(name="psum_a", bufs=5))
         ctx.enter_context(tc.manual_schedule())
 
+        zeros_f = keep.tile([P, P], F32, name="zeros_f")
+        nc.vector.memset(zeros_f[:], 0.0)
         ident_f = keep.tile([P, P], F32, name="ident_f")
         make_identity(nc, ident_f[:])
         ones = keep.tile([P, P], BF16, name="ones")
@@ -54,12 +56,13 @@ def tile_linearlayer_kernel(tc, x0e, x1o, x2e, w0e, w1o, w2e, bias, out):
         nc.vector.memset(warm_in[:], 0.0)
         warm_out = keep.tile([P, 8], F32, name="warm_out")
         nc.scalar.copy(out=warm_out[:], in_=warm_in[:])
-        if WARM:
-            zeros = keep.tile([P, 512], BF16, name="zeros")
-            nc.vector.memset(zeros[:], 0.0)
-            for i in range(WARM):
+
+        def feed_clock(count):
+            for i in range(count):
                 dummy = psum_a.tile([P, 512], F32, name="acc", tag="acc")
-                nc.tensor.matmul(out=dummy[:], lhsT=ones[:], rhs=zeros[:], start=True, stop=True)
+                nc.tensor.matmul(out=dummy[:, 0:P], lhsT=zeros_f[:], rhs=zeros_f[:], start=True, stop=True)
+
+        feed_clock(WARM)
 
         x0_view = x0e.rearrange("(c t p) k o -> c p t (k o)", c=CHUNKS, t=2, p=P)
         x1_view = x1o.rearrange("(c p j) i m -> c p (j i m)", c=CHUNKS, p=P, j=2)
@@ -184,14 +187,19 @@ def tile_linearlayer_kernel(tc, x0e, x1o, x2e, w0e, w1o, w2e, bias, out):
                 transpose_blocks(x_pair[c][:].bitcast(F32), first, count, x_t[c][:].bitcast(F32))
 
         transpose_k(w0_raw[0], w0_grouped[:, 0:1024])
+        feed_clock(1)
         pair_rows("v", w1_pair[:], w1_raw[:], D1, 0, 2)
         pair_rows("v", w1_pair[:], w1_raw[:], D1, 2, 3)
         transpose_k(w0_raw[1], w0_grouped[:, 1024:2048])
+        feed_clock(1)
         quantize_w0(0)
         transpose_k(x0_raw[0], x0_grouped[0][:])
+        feed_clock(1)
         quantize_w0(1)
         transpose_blocks(w1_pair[:].bitcast(F32), 0, 4, w1_t[:].bitcast(F32))
+        feed_clock(1)
         transpose_blocks(w1_pair[:].bitcast(F32), 4, 2, w1_t[:].bitcast(F32))
+        feed_clock(1)
         first_pieces = pair_pieces(0)
         first_pieces[0]()
         first_pieces[1]()
@@ -201,6 +209,7 @@ def tile_linearlayer_kernel(tc, x0e, x1o, x2e, w0e, w1o, w2e, bias, out):
         for m in range(D2):
             nc.tensor.transpose(bank_b[:, m * P : (m + 1) * P], w2_raw[:, m : W2 : D2], ident_b[:])
         nc.scalar.copy(out=w2_t[:], in_=bank_b[:])
+        feed_clock(1)
         for piece in first_pieces[2:]:
             piece()
 
@@ -210,6 +219,7 @@ def tile_linearlayer_kernel(tc, x0e, x1o, x2e, w0e, w1o, w2e, bias, out):
 
         for b in range(1, 4):
             t_bank(0, b)
+            feed_clock(1)
         for piece in pair_pieces(1):
             piece()
 

@@ -180,7 +180,6 @@ def tile_linearlayer_kernel(tc, x0e, x1o, x2e, w0e, w1o, w2e, bias, out):
         def t_bank(c, b):
             if b == 0:
                 transpose_k(x0_raw[c], x0_grouped[c][:])
-                quantize(x0_grouped[c][:], x0_codes[c][:], x0_scales[c][:])
             else:
                 first = 4 * (b - 1)
                 count = min(4, NB1 + NB2 - first)
@@ -285,18 +284,20 @@ def tile_linearlayer_kernel(tc, x0e, x1o, x2e, w0e, w1o, w2e, bias, out):
             pieces = pair_pieces(c + 2) if c + 2 < CHUNKS else []
             per_slot = (len(pieces) + 3) // 4
             for h in range(2):
-                for piece in pieces[(2 * h) * per_slot : (2 * h + 1) * per_slot]:
-                    piece()
                 if nxt:
                     t_bank(c + 1, 2 * h)
                 group_1o(c, h, 0)
                 mx_group(c, h)
                 group_1o(c, h, 1)
                 store(c, h, 0, Y2)
-                for piece in pieces[(2 * h + 1) * per_slot : (2 * h + 2) * per_slot]:
+                if nxt and h == 0:
+                    quantize(x0_grouped[c + 1][:], x0_codes[c + 1][:], x0_scales[c + 1][:])
+                for piece in pieces[(2 * h) * per_slot : (2 * h + 1) * per_slot]:
                     piece()
                 if nxt:
                     t_bank(c + 1, 2 * h + 1)
                 group_2e(c, h, 0)
                 group_2e(c, h, 1)
                 store(c, h, Y2, WIDTH)
+                for piece in pieces[(2 * h + 1) * per_slot : (2 * h + 2) * per_slot]:
+                    piece()

@@ -108,8 +108,8 @@ def tile_linearlayer_kernel(tc, x0e, x1o, x2e, w0e, w1o, w2e, bias, out):
             nc.sync.dma_start(out=x2_raw[c][:], in_=x2_view[c, :, :])
 
         load_w0(0)
-        nc.sync.dma_start(out=w1_raw[:], in_=w1o.rearrange("(p j) i m -> p (j i m)", j=2))
         load_w0(1)
+        nc.sync.dma_start(out=w1_raw[:], in_=w1o.rearrange("(p j) i m -> p (j i m)", j=2))
         load_x0(0)
         load_x1(0)
         nc.sync.dma_start(out=w2_raw[:], in_=w2e.rearrange("o i m -> o (i m)"))

from contextlib import ExitStack

import concourse.mybir as mybir
from concourse.masks import make_identity

F32 = mybir.dt.float32
BF16 = mybir.dt.bfloat16
U32 = mybir.dt.uint32
U8 = mybir.dt.uint8
FP8X4 = mybir.dt.float8_e5m2_x4
ADD = mybir.AluOpType.add
MULT = mybir.AluOpType.mult

P = 128
ROWS = 1024
CHUNKS = 4
K0 = 512
O0 = 512
I1, O1, D1 = 256, 256, 3
I2, O2, D2 = 128, 128, 5
W1 = I1 * D1
W2 = I2 * D2
NB1 = 6
NB2 = 5
Y1 = O0
Y2 = O0 + O1 * D1
WIDTH = Y2 + O2 * D2

POOL_CHUNKS = ()
WARM = 7
ACT_2E = ((0, 0),)
DVE_1O = ()

FLOPS = 2 * ROWS * (K0 * O0 + D1 * I1 * O1 + D2 * I2 * O2)


def tile_linearlayer_kernel(tc, x0e, x1o, x2e, w0e, w1o, w2e, bias, out):
    nc = tc.nc
    with ExitStack() as ctx:
        keep = ctx.enter_context(tc.tile_pool(name="keep", bufs=1))
        psum_t = ctx.enter_context(tc.psum_pool(name="psum_t", bufs=3))
        psum_a = ctx.enter_context(tc.psum_pool(name="psum_a", bufs=5))
        ctx.enter_context(tc.manual_schedule())

        zeros_f = keep.tile([P, P], F32, name="zeros_f")
        nc.vector.memset(zeros_f[:], 0.0)
        ident_f = keep.tile([P, P], F32, name="ident_f")
        make_identity(nc, ident_f[:])
        ones = keep.tile([P, P], BF16, name="ones")
        nc.gpsimd.memset(ones[:], 1.0)
        ident_b = keep.tile([P, P], BF16, name="ident_b")
        make_identity(nc, ident_b[:])
        bias_row = keep.tile([P, O0], BF16, name="bias_row")
        nc.vector.memset(bias_row[:], 0.0)
        warm_in = keep.tile([P, 8], F32, name="warm_in")
        nc.vector.memset(warm_in[:], 0.0)
        warm_out = keep.tile([P, 8], F32, name="warm_out")
        nc.scalar.copy(out=warm_out[:], in_=warm_in[:])

        def feed_clock(count):
            for i in range(count):
                dummy = psum_a.tile([P, 512], F32, name="acc", tag="acc")
                nc.tensor.matmul(out=dummy[:, 0:P], lhsT=zeros_f[:], rhs=zeros_f[:], start=True, stop=True)

        feed_clock(WARM)

        x0_view = x0e.rearrange("(c t p) k o -> c p t (k o)", c=CHUNKS, t=2, p=P)
        x1_view = x1o.rearrange("(c p j) i m -> c p (j i m)", c=CHUNKS, p=P, j=2)
        x2_view = x2e.rearrange("(c p j) i m -> c p (j i m)", c=CHUNKS, p=P, j=2)
        w0_view = w0e.rearrange("(b t p) k o -> b p t (k o)", b=2, t=2, p=P)

        w0_raw = []
        for b in range(2):
            w0_raw.append(keep.tile([P, 2, K0], BF16, name="w0_raw%d" % b))
        x0_raw, x1_raw, x2_raw = [], [], []
        x0_grouped, x0_codes, x0_scales, x_pair, x_t, o_tiles = [], [], [], [], [], []
        for c in range(CHUNKS):
            x0_raw.append(keep.tile([P, 2, K0], BF16, name="x0_raw%d" % c))
            x1_raw.append(keep.tile([P, 2 * W1], BF16, name="x1_raw%d" % c))
            x2_raw.append(keep.tile([P, 2 * W2], BF16, name="x2_raw%d" % c))
            x0_grouped.append(keep.tile([P, 1024], BF16, name="x0_grouped%d" % c, align_bytes=64))
            x0_codes.append(keep.tile([P, 256], U32, name="x0_codes%d" % c, align_bytes=64))
            x0_scales.append(keep.tile([P, 256], U8, name="x0_scales%d" % c, align_bytes=64))
            x_pair.append(keep.tile([P, 2 * (W1 + W2)], BF16, name="x_pair%d" % c))
            x_t.append(keep.tile([P, 2 * (W1 + W2)], BF16, name="x_t%d" % c))
            for h in range(2):
                o_tiles.append(keep.tile([P, WIDTH], F32, name="o_%d_%d" % (c, h)))
        w1_raw = keep.tile([P, 2 * W1], BF16, name="w1_raw")
        w2_raw = keep.tile([P, W2], BF16, name="w2_raw")
        w1_pair = keep.tile([P, 2 * W1], BF16, name="w1_pair")
        w0_grouped = keep.tile([P, 4 * O0], BF16, name="w0_grouped", align_bytes=64)
        w0_codes = keep.tile([P, O0], U32, name="w0_codes", align_bytes=64)
        w0_scales = keep.tile([P, O0], U8, name="w0_scales", align_bytes=64)
        w2_t = keep.tile([P, W2], BF16, name="w2_t")
        w1_t = keep.tile([P, 2 * W1], BF16, name="w1_t")
        bias_bc = keep.tile([P, O0], F32, name="bias_bc")

        def load_w0(b):
            nc.sync.dma_start(out=w0_raw[b][:], in_=w0_view[b, :, :, :])

        def load_x0(c):
            nc.sync.dma_start(out=x0_raw[c][:], in_=x0_view[c, :, :, :])

        def load_x1(c):
            nc.sync.dma_start(out=x1_raw[c][:], in_=x1_view[c, :, :])

        def load_x2(c):
            nc.sync.dma_start(out=x2_raw[c][:], in_=x2_view[c, :, :])

        load_w0(0)
        load_w0(1)
        nc.sync.dma_start(out=w1_raw[:], in_=w1o.rearrange("(p j) i m -> p (j i m)", j=2))
        load_x0(0)
        load_x1(0)
        nc.sync.dma_start(out=w2_raw[:], in_=w2e.rearrange("o i m -> o (i m)"))
        load_x2(0)
        nc.sync.dma_start(out=bias_row[0:1, :], in_=bias.rearrange("(a n) -> a n", a=1))
        for c in range(1, CHUNKS):
            load_x1(c)
            load_x2(c)
            load_x0(c)

        def pair_rows(eng, dst, src, comps, m0, m1):
            per = dst.shape[1] // comps
            o_ap = dst[:, m0 * per : m1 * per].rearrange("p (m i j) -> p m i j", m=m1 - m0, j=2)
            i_ap = src.rearrange("p (j i m) -> p m i j", j=2, m=comps)[:, m0:m1]
            if eng == "v":
                nc.vector.tensor_copy(out=o_ap, in_=i_ap)
            elif eng == "a":
                nc.scalar.copy(out=o_ap, in_=i_ap)
            else:
                nc.gpsimd.tensor_scalar(out=o_ap, in0=i_ap, scalar1=1.0, scalar2=0.0, op0=MULT, op1=ADD)

        def pair_pieces(c):
            d1 = x_pair[c][:, 0 : 2 * W1]
            d2 = x_pair[c][:, 2 * W1 : 2 * (W1 + W2)]
            s1 = x1_raw[c][:]
            s2 = x2_raw[c][:]
            if c in POOL_CHUNKS:
                return [
                    lambda: pair_rows("g", d1, s1, D1, 0, D1),
                    lambda: pair_rows("g", d2, s2, D2, 0, D2),
                ]
            return [
                lambda: pair_rows("v", d1, s1, D1, 0, 2),
                lambda: pair_rows("v", d1, s1, D1, 2, 3),
                lambda: pair_rows("v", d2, s2, D2, 0, 4),
                lambda: pair_rows("v", d2, s2, D2, 4, 5),
            ]

        def transpose_blocks(src_words, first, count, dst_words):
            bank = psum_t.tile([P, 512], F32, name="tp", tag="tp")
            for q in range(count):
                k = first + q
                nc.tensor.transpose(bank[:, q * P : (q + 1) * P], src_words[:, k * P : (k + 1) * P], ident_f[:])
            nc.scalar.copy(out=dst_words[:, first * P : (first + count) * P], in_=bank[:, 0 : count * P])

        def transpose_k(src, grouped):
            words = src[:].bitcast(F32)
            bank = psum_t.tile([P, 512], F32, name="tp", tag="tp")
            for t in range(2):
                for u in range(2):
                    q = 2 * t + u
                    nc.tensor.transpose(bank[:, q * P : (q + 1) * P], words[:, t, u : K0 // 2 : 2], ident_f[:])
            nc.scalar.copy(
                out=grouped.bitcast(F32).rearrange("p (t n u) -> p t n u", t=2, u=2),
                in_=bank[:].rearrange("p (t u n) -> p t n u", t=2, u=2),
            )

        def quantize(grouped, codes, scales):
            nc.vector.quantize_mx(out=codes.bitcast(FP8X4), scales=scales, in_=grouped)

        def quantize_w0(b):
            quantize(
                w0_grouped[:, b * 1024 : (b + 1) * 1024],
                w0_codes[:, b * 256 : (b + 1) * 256],
                w0_scales[:, b * 256 : (b + 1) * 256],
            )

        def t_bank(c, b):
            if b == 0:
                transpose_k(x0_raw[c], x0_grouped[c][:])
            else:
                first = 4 * (b - 1)
                count = min(4, NB1 + NB2 - first)
                transpose_blocks(x_pair[c][:].bitcast(F32), first, count, x_t[c][:].bitcast(F32))

        transpose_k(w0_raw[0], w0_grouped[:, 0:1024])
        feed_clock(1)
        pair_rows("v", w1_pair[:], w1_raw[:], D1, 0, 2)
        pair_rows("v", w1_pair[:], w1_raw[:], D1, 2, 3)
        transpose_k(w0_raw[1], w0_grouped[:, 1024:2048])
        feed_clock(1)
        quantize_w0(0)
        transpose_k(x0_raw[0], x0_grouped[0][:])
        feed_clock(1)
        quantize_w0(1)
        transpose_blocks(w1_pair[:].bitcast(F32), 0, 4, w1_t[:].bitcast(F32))
        feed_clock(1)
        transpose_blocks(w1_pair[:].bitcast(F32), 4, 2, w1_t[:].bitcast(F32))
        feed_clock(1)
        first_pieces = pair_pieces(0)
        first_pieces[0]()
        first_pieces[1]()
        quantize(x0_grouped[0][:], x0_codes[0][:], x0_scales[0][:])

        bank_b = psum_t.tile([P, W2], BF16, name="tpb", tag="tp")
        for m in range(D2):
            nc.tensor.transpose(bank_b[:, m * P : (m + 1) * P], w2_raw[:, m : W2 : D2], ident_b[:])
        nc.scalar.copy(out=w2_t[:], in_=bank_b[:])
        feed_clock(1)
        for piece in first_pieces[2:]:
            piece()

        bias_ps = psum_a.tile([P, 512], F32, name="acc", tag="acc")
        nc.tensor.matmul(out=bias_ps[:], lhsT=ones[:], rhs=bias_row[:], start=True, stop=True)
        nc.vector.tensor_copy(out=bias_bc[:], in_=bias_ps[:])

        for b in range(1, 4):
            t_bank(0, b)
            feed_clock(1)
        for piece in pair_pieces(1):
            piece()

        def mx_group(c, h):
            acc = psum_a.tile([P, 512], F32, name="acc", tag="acc")
            cols = slice(h * P, (h + 1) * P)
            nc.tensor.matmul_mx(
                out=acc[:],
                lhsT=x0_codes[c][:, cols].bitcast(FP8X4),
                lhsT_scale=x0_scales[c][:, cols],
                rhs=w0_codes[:].bitcast(FP8X4),
                rhs_scale=w0_scales[:],
                start=True,
                stop=True,
            )
            nc.vector.tensor_tensor(out=o_tiles[2 * c + h][:, 0:O0], in0=acc[:], in1=bias_bc[:], op=ADD)

        def group_1o(c, h, g):
            acc = psum_a.tile([P, 512], F32, name="acc", tag="acc")
            for m in range(D1):
                for ib in range(2):
                    k = 2 * m + ib
                    nc.tensor.matmul(
                        out=acc[:, m * P : (m + 1) * P],
                        lhsT=x_t[c][:, k * 256 + h * P : k * 256 + (h + 1) * P],
                        rhs=w1_t[:, k * 256 + g * P : k * 256 + (g + 1) * P],
                        start=(ib == 0),
                        stop=(ib == 1),
                    )
            n = D1 * P
            dst = o_tiles[2 * c + h][:, Y1 + g * n : Y1 + (g + 1) * n]
            src = acc[:, 0:n].rearrange("p (m o) -> p o m", m=D1)
            if (h, g) in DVE_1O:
                nc.vector.tensor_copy(out=dst, in_=src)
            else:
                nc.scalar.copy(out=dst, in_=src)

        def group_2e(c, h, g):
            acc = psum_a.tile([P, 512], F32, name="acc", tag="acc")
            for m in range(D2):
                k = NB1 + m
                nc.tensor.matmul(
                    out=acc[:, m * 64 : (m + 1) * 64],
                    lhsT=x_t[c][:, k * 256 + h * P : k * 256 + (h + 1) * P],
                    rhs=w2_t[:, m * P + g * 64 : m * P + (g + 1) * 64],
                    start=True,
                    stop=True,
                )
            n = D2 * 64
            dst = o_tiles[2 * c + h][:, Y2 + g * n : Y2 + (g + 1) * n]
            src = acc[:, 0:n].rearrange("p (m o) -> p o m", m=D2)
            if (h, g) in ACT_2E:
                nc.scalar.copy(out=dst, in_=src)
            else:
                nc.vector.tensor_copy(out=dst, in_=src)

        def store(c, h, lo, hi):
            r0 = (2 * c + h) * P
            nc.sync.dma_start(out=out[r0 : r0 + P, lo:hi], in_=o_tiles[2 * c + h][:, lo:hi])

        for c in range(CHUNKS):
            nxt = c + 1 < CHUNKS
            pieces = pair_pieces(c + 2) if c + 2 < CHUNKS else []
            per_slot = (len(pieces) + 3) // 4
            for h in range(2):
                if nxt:
                    t_bank(c + 1, 2 * h)
                group_1o(c, h, 0)
                mx_group(c, h)
                group_1o(c, h, 1)
                store(c, h, 0, Y2)
                if nxt and h == 0:
                    quantize(x0_grouped[c + 1][:], x0_codes[c + 1][:], x0_scales[c + 1][:])
                for piece in pieces[(2 * h) * per_slot : (2 * h + 1) * per_slot]:
                    piece()
                if nxt:
                    t_bank(c + 1, 2 * h + 1)
                group_2e(c, h, 0)
                group_2e(c, h, 1)
                store(c, h, Y2, WIDTH)
                for piece in pieces[(2 * h + 1) * per_slot : (2 * h + 2) * per_slot]:
                    piece()
